import numpy as np
import ml_dtypes


def mxq(x, axis, fmt="e4m3"):
    dtype, down = {"e4m3": (ml_dtypes.float8_e4m3fn, 7), "e5m2": (ml_dtypes.float8_e5m2, 14)}[fmt]
    v = np.moveaxis(np.asarray(x, np.float32).astype(ml_dtypes.bfloat16).astype(np.float64), axis, -1)
    blocks = v.reshape(v.shape[:-1] + (-1, 32))
    amax = np.abs(blocks).max(-1, keepdims=True)
    byte = np.maximum(np.where(amax > 0, np.frexp(amax)[1] - 1 + 127, 0) - down, 1)
    scale = np.exp2(byte - 127.0)
    codes = (blocks / scale).astype(np.float32).astype(dtype).astype(np.float64)
    return np.moveaxis((codes * scale).reshape(v.shape), -1, axis)


WIDE = False


def mx_kscale(k):
    if not WIDE:
        return np.ones(k)
    levels = np.array([10, -10, 5, -5, 0])
    a = np.random.permutation(np.resize(levels, k // 512 * 4)).reshape(k // 512, 4)
    idx = np.arange(k)
    return np.exp2(a[idx // 512, idx % 128 // 32])


BF16 = ml_dtypes.bfloat16


def bf(x):
    return np.asarray(x, np.float32).astype(BF16)


def f64(x):
    return np.asarray(x).astype(np.float64)


E2M1 = np.array([0.0, 0.5, 1.0, 1.5, 2.0, 3.0, 4.0, 6.0, -0.0, -0.5, -1.0, -1.5, -2.0, -3.0, -4.0, -6.0])


def pack_weight(w, fmt):
    k, n = w.shape
    w = f64(bf(w)).reshape(k // 32, 32, n)
    amax = np.abs(w).max(1)
    if fmt == "e4m3":
        byte = np.frexp(amax)[1] - 1 + 127 - 7
    else:
        mant, ex = np.frexp(amax / 6.0)
        byte = np.where(mant > 0.5, ex, ex - 1) + 127
    byte = np.clip(np.where(amax > 0, byte, 1), 1, 254)
    scaled = (w * np.exp2(127.0 - byte)[:, None, :]).reshape(k, n).astype(np.float32)
    by_word = np.ascontiguousarray(scaled.reshape(k // 512, 128, 4, n).transpose(0, 1, 3, 2))
    if fmt == "e4m3":
        words = by_word.astype(ml_dtypes.float8_e4m3fn).view(np.uint8)
    else:
        c = by_word.astype(ml_dtypes.float4_e2m1fn).view(np.uint8) & 0xF
        words = c[..., 0::2] | (c[..., 1::2] << 4)
    return np.ascontiguousarray(words), np.ascontiguousarray(byte.astype(np.uint8).reshape(k // 512, 16, n))


def unpack_weight(words, scales, fmt):
    g, p, n, _ = words.shape
    if fmt == "e4m3":
        vals = np.ascontiguousarray(words).view(ml_dtypes.float8_e4m3fn).astype(np.float64)
    else:
        nib = np.empty((g, p, n, 4), np.uint8)
        nib[..., 0::2] = words & 0xF
        nib[..., 1::2] = words >> 4
        vals = E2M1[nib]
    vals = vals * np.repeat(np.exp2(scales.astype(np.float64) - 127.0), 8, axis=1)[..., None]
    return vals.transpose(0, 1, 3, 2).reshape(g * 512, n)

def pack4(w):
    words, scales = pack_weight(w, "e2m1")
    return words.reshape(words.shape[0], 128, -1), scales


def unpack4(words, scales):
    return unpack_weight(words.reshape(words.shape[0], 128, -1, 2), scales, "e2m1")


B, L, F, D, N = 16, 1024, 512, 512, 8192
TOP = 0.8 * np.sqrt(2.0 * np.log(L))


def elu(v):
    return np.where(v > 0.0, v, np.exp(np.minimum(v, 0.0)) - 1.0)


def setup_inputs():
    s = mx_kscale(F)
    x = bf(np.random.standard_normal((B, L, F)) * s)
    words, scales = pack4((np.random.standard_normal((D, F)) / np.sqrt(F) / s).T)
    conv_b = bf(np.random.standard_normal(D) * 2.0 - TOP)
    return {"x": x,
            "conv_w_words": words,
            "conv_w_scales": scales,
            "conv_b": conv_b}


def reference(x, conv_w_words, conv_w_scales, conv_b):
    z = (mxq(f64(x), 2, "e4m3") @ unpack4(conv_w_words, conv_w_scales)) + f64(conv_b)
    return elu(z).max(axis=1)

@@ -1,0 +1,173 @@
+from contextlib import ExitStack
+
+import concourse.mybir as mybir
+from concourse.masks import make_identity
+
+F32 = mybir.dt.float32
+BF16 = mybir.dt.bfloat16
+I32 = mybir.dt.int32
+U32 = mybir.dt.uint32
+U8 = mybir.dt.uint8
+FP8X4 = mybir.dt.float8_e4m3fn_x4
+FP4X4 = mybir.dt.float4_e2m1fn_x4
+ALU = mybir.AluOpType
+ACT = mybir.ActivationFunctionType
+AXIS = mybir.AxisListType
+
+SEQS, POSITIONS, FEATURES, OUT_FEATURES = 16, 1024, 512, 512
+P = 128
+PACK = 4
+PAIR = 2
+ROUND = 512
+ROW_TILES = ROUND // P
+ROUNDS_PER_SEQ = POSITIONS // ROUND
+ROUNDS = SEQS * ROUNDS_PER_SEQ
+D_TILES = OUT_FEATURES // P
+BANK_F32 = 512
+TILES_PER_BANK = BANK_F32 // (PAIR * P)
+X_BUFS = 8
+RESULT_ROWS = SEQS * D_TILES
+
+FLOPS = 2 * SEQS * POSITIONS * FEATURES * OUT_FEATURES
+
+
+def tile_conceptembedmodel_pa_t_kernel(tc, x, conv_w_words, conv_w_scales, conv_b, out):
+    nc = tc.nc
+    x_rounds = x.rearrange(
+        "b (h p j) f -> (b h) p (j f)", h=ROUNDS_PER_SEQ, p=P, j=ROW_TILES
+    )
+
+    with ExitStack() as stack:
+        stack.enter_context(tc.manual_schedule())
+        const = stack.enter_context(tc.tile_pool(name="const", bufs=1))
+        x_pool = stack.enter_context(tc.tile_pool(name="x", bufs=X_BUFS))
+        stage = stack.enter_context(tc.tile_pool(name="stage", bufs=3))
+        xt_pool = stack.enter_context(tc.psum_pool(name="xt", bufs=2))
+        z_pool = stack.enter_context(tc.psum_pool(name="z", bufs=6))
+
+        x_tiles = {}
+        grouped_tiles = {}
+        code_tiles = {}
+        z_tiles = {}
+
+        def load(r):
+            x_sb = x_pool.tile([P, ROW_TILES * FEATURES], BF16, name="x_sb")
+            nc.sync.dma_start(out=x_sb[:], in_=x_rounds[r])
+            x_tiles[r] = x_sb
+
+        def transpose_and_regroup(r):
+            words = x_tiles[r][:].bitcast(F32).rearrange(
+                "p (j w u) -> p j u w", j=ROW_TILES, u=PAIR
+            )
+            grouped = stage.tile([P, ROUND * PACK], BF16, name="grouped", align_bytes=64)
+            grouped_words = grouped[:].bitcast(F32).rearrange("p (l u) -> p l u", u=PAIR)
+            banks = []
+            for first in range(0, ROW_TILES, TILES_PER_BANK):
+                xt = xt_pool.tile([P, PAIR, TILES_PER_BANK * P], F32, name="xt")
+                for i in range(TILES_PER_BANK):
+                    for u in range(PAIR):
+                        nc.tensor.transpose(
+                            xt[:, u, i * P : (i + 1) * P], words[:, first + i, u, :], identity[:]
+                        )
+                banks.append((first, xt))
+            for first, xt in banks:
+                nc.scalar.copy(
+                    out=grouped_words[:, first * P : (first + TILES_PER_BANK) * P, :],
+                    in_=xt[:].rearrange("p u l -> p l u"),
+                )
+            grouped_tiles[r] = grouped
+
+        def quantise(r):
+            codes = stage.tile([P, ROUND], U32, name="codes", align_bytes=64)
+            scales = stage.tile([P, ROUND], U8, name="scales", align_bytes=64)
+            nc.vector.quantize_mx(
+                out=codes[:].bitcast(FP8X4), scales=scales[:], in_=grouped_tiles[r][:]
+            )
+            code_tiles[r] = (codes, scales)
+
+        def multiply(r, t):
+            codes, scales = code_tiles[r]
+            z = z_pool.tile([P, ROUND], F32, name="z")
+            nc.tensor.matmul_mx(
+                out=z[:],
+                lhsT=w_words[:, t * PAIR * P : (t + 1) * PAIR * P].bitcast(FP4X4),
+                lhsT_scale=w_scales[:, t * P : (t + 1) * P],
+                rhs=codes[:].bitcast(FP8X4),
+                rhs_scale=scales[:],
+                start=True,
+                stop=True,
+            )
+            z_tiles[(r, t)] = z
+
+        def take_max(r, t):
+            b, h = divmod(r, ROUNDS_PER_SEQ)
+            nc.vector.reduce_max(
+                out=round_max[:, b, t, h : h + 1], in_=z_tiles[(r, t)][:], axis=AXIS.X
+            )
+
+        w_scales = const.tile([P, OUT_FEATURES], U8, name="w_scales", align_bytes=64)
+        nc.vector.memset(w_scales[:].bitcast(I32), 0)
+        seq_max = const.tile([P, P], F32, name="seq_max")
+        nc.vector.memset(seq_max[:], 0.0)
+        warm = const.tile([P, 1], F32, name="warm")
+        nc.vector.memset(warm[:], 0.0)
+        nc.scalar.activation(out=warm[:], in_=warm[:], func=ACT.Exp)
+        identity = const.tile([P, P], F32, name="identity")
+        make_identity(nc, identity[:])
+        round_max = const.tile([P, SEQS, D_TILES, ROUNDS_PER_SEQ], F32, name="round_max")
+
+        load(0)
+        w_words = const.tile([P, PAIR * OUT_FEATURES], U8, name="w_words", align_bytes=64)
+        nc.sync.dma_start(out=w_words[:].bitcast(I32), in_=conv_w_words[0].bitcast(I32))
+        for quadrant in range(4):
+            nc.sync.dma_start(
+                out=w_scales[32 * quadrant : 32 * quadrant + 4, :].bitcast(I32),
+                in_=conv_w_scales[0, 4 * quadrant : 4 * quadrant + 4, :].bitcast(I32),
+            )
+        bias_rows = const.tile([RESULT_ROWS, P], BF16, name="bias_rows")
+        nc.sync.dma_start(
+            out=bias_rows[:],
+            in_=conv_b.rearrange("(o t d) -> o t d", o=1, t=D_TILES).to_broadcast(
+                [SEQS, D_TILES, P]
+            ),
+        )
+        for r in range(1, X_BUFS):
+            load(r)
+
+        transpose_and_regroup(0)
+        quantise(0)
+        transpose_and_regroup(1)
+        for t in range(D_TILES):
+            multiply(0, t)
+        for r in range(ROUNDS):
+            if r + X_BUFS < ROUNDS:
+                load(r + X_BUFS)
+            if r + 2 < ROUNDS:
+                transpose_and_regroup(r + 2)
+            if r + 1 < ROUNDS:
+                quantise(r + 1)
+            for t in range(D_TILES):
+                if r + 1 < ROUNDS:
+                    multiply(r + 1, t)
+                take_max(r, t)
+
+        nc.vector.reduce_max(
+            out=seq_max[:, 0:RESULT_ROWS].rearrange("p (b t) -> p b t", t=D_TILES),
+            in_=round_max[:],
+            axis=AXIS.X,
+        )
+        rows = xt_pool.tile([P, P], F32, name="rows", tag="xt")
+        nc.tensor.transpose(rows[:], seq_max[:], identity[:])
+        v = const.tile([RESULT_ROWS, P], F32, name="v")
+        nc.vector.tensor_tensor(out=v[:], in0=rows[0:RESULT_ROWS, :], in1=bias_rows[:], op=ALU.add)
+        negative = const.tile([RESULT_ROWS, P], F32, name="negative")
+        nc.vector.tensor_scalar_min(negative[:], v[:], 0.0)
+        grown = const.tile([RESULT_ROWS, P], F32, name="grown")
+        nc.scalar.activation(out=grown[:], in_=negative[:], func=ACT.Exp)
+        positive = const.tile([RESULT_ROWS, P], F32, name="positive")
+        nc.vector.tensor_scalar_max(positive[:], v[:], 0.0)
+        result = const.tile([RESULT_ROWS, P], F32, name="result")
+        nc.vector.scalar_tensor_tensor(
+            out=result[:], in0=grown[:], scalar=-1.0, in1=positive[:], op0=ALU.add, op1=ALU.add
+        )
+        nc.sync.dma_start(out=out.rearrange("b (t d) -> (b t) d", t=D_TILES), in_=result[:])

@@ -41,7 +41,7 @@ def tile_conceptembedmodel_pa_t_kernel(tc, x, conv_w_words, conv_w_scales, conv_
         stack.enter_context(tc.manual_schedule())
         const = stack.enter_context(tc.tile_pool(name="const", bufs=1))
         x_pool = stack.enter_context(tc.tile_pool(name="x", bufs=X_BUFS))
-        stage = stack.enter_context(tc.tile_pool(name="stage", bufs=3))
+        stage = stack.enter_context(tc.tile_pool(name="stage", bufs=4))
         xt_pool = stack.enter_context(tc.psum_pool(name="xt", bufs=2))
         z_pool = stack.enter_context(tc.psum_pool(name="z", bufs=6))
 
@@ -139,17 +139,23 @@ def tile_conceptembedmodel_pa_t_kernel(tc, x, conv_w_words, conv_w_scales, conv_
         transpose_and_regroup(1)
         for t in range(D_TILES):
             multiply(0, t)
+        transpose_and_regroup(2)
         for r in range(ROUNDS):
             if r + X_BUFS < ROUNDS:
                 load(r + X_BUFS)
-            if r + 2 < ROUNDS:
-                transpose_and_regroup(r + 2)
             if r + 1 < ROUNDS:
                 quantise(r + 1)
-            for t in range(D_TILES):
-                if r + 1 < ROUNDS:
-                    multiply(r + 1, t)
-                take_max(r, t)
+                multiply(r + 1, 0)
+                multiply(r + 1, 1)
+            if r + 3 < ROUNDS:
+                transpose_and_regroup(r + 3)
+            take_max(r, 0)
+            take_max(r, 1)
+            if r + 1 < ROUNDS:
+                multiply(r + 1, 2)
+                multiply(r + 1, 3)
+            take_max(r, 2)
+            take_max(r, 3)
 
         nc.vector.reduce_max(
             out=seq_max[:, 0:RESULT_ROWS].rearrange("p (b t) -> p b t", t=D_TILES),

@@ -27,6 +27,9 @@ BANK_F32 = 512
 TILES_PER_BANK = BANK_F32 // (PAIR * P)
 X_BUFS = 8
 RESULT_ROWS = SEQS * D_TILES
+HANDED_TILE = D_TILES - 1
+HANDED_SEQS = 13
+HALF = ROUND // 2
 
 FLOPS = 2 * SEQS * POSITIONS * FEATURES * OUT_FEATURES
 
@@ -44,11 +47,16 @@ def tile_conceptembedmodel_pa_t_kernel(tc, x, conv_w_words, conv_w_scales, conv_
         stage = stack.enter_context(tc.tile_pool(name="stage", bufs=4))
         xt_pool = stack.enter_context(tc.psum_pool(name="xt", bufs=2))
         z_pool = stack.enter_context(tc.psum_pool(name="z", bufs=6))
+        handed = stack.enter_context(tc.tile_pool(name="handed", bufs=4))
 
         x_tiles = {}
         grouped_tiles = {}
         code_tiles = {}
         z_tiles = {}
+        half_tiles = {}
+        difference_tiles = {}
+        excess_tiles = {}
+        joined_tiles = {}
 
         def load(r):
             x_sb = x_pool.tile([P, ROW_TILES * FEATURES], BF16, name="x_sb")
@@ -105,6 +113,43 @@ def tile_conceptembedmodel_pa_t_kernel(tc, x, conv_w_words, conv_w_scales, conv_
                 out=round_max[:, b, t, h : h + 1], in_=z_tiles[(r, t)][:], axis=AXIS.X
             )
 
+        def hand_over(r):
+            s, h = divmod(r, ROUNDS_PER_SEQ)
+            half = handed.tile([P, ROUND], F32, name="half%d" % h)
+            nc.scalar.copy(out=half[:], in_=z_tiles[(r, HANDED_TILE)][:])
+            half_tiles[(s, h)] = half
+
+        def wait_for_quantise(r):
+            token = handed.tile([P, 1], U32, name="token")
+            nc.gpsimd.tensor_copy(out=token[:], in_=code_tiles[r][0][:, 0:1])
+
+        def subtract(s):
+            difference = handed.tile([P, ROUND], F32, name="difference")
+            nc.gpsimd.tensor_tensor(
+                out=difference[:], in0=half_tiles[(s, 0)][:], in1=half_tiles[(s, 1)][:],
+                op=ALU.subtract,
+            )
+            difference_tiles[s] = difference
+
+        def relu(s):
+            excess = handed.tile([P, ROUND], F32, name="excess")
+            nc.scalar.activation(out=excess[:], in_=difference_tiles[s][:], func=ACT.Relu)
+            excess_tiles[s] = excess
+
+        def add(s):
+            joined = handed.tile([P, ROUND], F32, name="joined")
+            nc.gpsimd.tensor_tensor(
+                out=joined[:], in0=excess_tiles[s][:], in1=half_tiles[(s, 1)][:], op=ALU.add
+            )
+            joined_tiles[s] = joined
+
+        def take_joined_max(s, i):
+            nc.vector.reduce_max(
+                out=round_max[:, s, HANDED_TILE, i : i + 1],
+                in_=joined_tiles[s][:, i * HALF : (i + 1) * HALF],
+                axis=AXIS.X,
+            )
+
         w_scales = const.tile([P, OUT_FEATURES], U8, name="w_scales", align_bytes=64)
         nc.vector.memset(w_scales[:].bitcast(I32), 0)
         seq_max = const.tile([P, P], F32, name="seq_max")
@@ -141,21 +186,35 @@ def tile_conceptembedmodel_pa_t_kernel(tc, x, conv_w_words, conv_w_scales, conv_
             multiply(0, t)
         transpose_and_regroup(2)
         for r in range(ROUNDS):
+            is_handed = r // ROUNDS_PER_SEQ < HANDED_SEQS
             if r + X_BUFS < ROUNDS:
                 load(r + X_BUFS)
             if r + 1 < ROUNDS:
                 quantise(r + 1)
+                if r % 2 == 0 and 0 <= (r - 2) // 2 < HANDED_SEQS:
+                    wait_for_quantise(r + 1)
+                    subtract((r - 2) // 2)
+                if r % 2 == 1 and 0 <= (r - 5) // 2 < HANDED_SEQS:
+                    wait_for_quantise(r + 1)
+                    add((r - 5) // 2)
                 multiply(r + 1, 0)
                 multiply(r + 1, 1)
+            if is_handed:
+                hand_over(r)
+            if r % 2 == 1 and 0 <= (r - 3) // 2 < HANDED_SEQS:
+                relu((r - 3) // 2)
             if r + 3 < ROUNDS:
                 transpose_and_regroup(r + 3)
+            if 0 <= (r - 6) // 2 < HANDED_SEQS:
+                take_joined_max((r - 6) // 2, r % 2)
             take_max(r, 0)
             take_max(r, 1)
             if r + 1 < ROUNDS:
                 multiply(r + 1, 2)
                 multiply(r + 1, 3)
             take_max(r, 2)
-            take_max(r, 3)
+            if not is_handed:
+                take_max(r, 3)
 
         nc.vector.reduce_max(
             out=seq_max[:, 0:RESULT_ROWS].rearrange("p (b t) -> p b t", t=D_TILES),

@@ -28,7 +28,7 @@ TILES_PER_BANK = BANK_F32 // (PAIR * P)
 X_BUFS = 8
 RESULT_ROWS = SEQS * D_TILES
 HANDED_TILE = D_TILES - 1
-HANDED_SEQS = 13
+HANDED_SEQS = 15
 HALF = ROUND // 2
 
 FLOPS = 2 * SEQS * POSITIONS * FEATURES * OUT_FEATURES
@@ -51,6 +51,7 @@ def tile_conceptembedmodel_pa_t_kernel(tc, x, conv_w_words, conv_w_scales, conv_
 
         x_tiles = {}
         grouped_tiles = {}
+        xt_tiles = {}
         code_tiles = {}
         z_tiles = {}
         half_tiles = {}
@@ -63,13 +64,12 @@ def tile_conceptembedmodel_pa_t_kernel(tc, x, conv_w_words, conv_w_scales, conv_
             nc.sync.dma_start(out=x_sb[:], in_=x_rounds[r])
             x_tiles[r] = x_sb
 
-        def transpose_and_regroup(r):
+        def transpose(r):
             words = x_tiles[r][:].bitcast(F32).rearrange(
                 "p (j w u) -> p j u w", j=ROW_TILES, u=PAIR
             )
-            grouped = stage.tile([P, ROUND * PACK], BF16, name="grouped", align_bytes=64)
-            grouped_words = grouped[:].bitcast(F32).rearrange("p (l u) -> p l u", u=PAIR)
-            banks = []
+            grouped_tiles[r] = stage.tile([P, ROUND * PACK], BF16, name="grouped", align_bytes=64)
+            xt_tiles[r] = []
             for first in range(0, ROW_TILES, TILES_PER_BANK):
                 xt = xt_pool.tile([P, PAIR, TILES_PER_BANK * P], F32, name="xt")
                 for i in range(TILES_PER_BANK):
@@ -77,13 +77,20 @@ def tile_conceptembedmodel_pa_t_kernel(tc, x, conv_w_words, conv_w_scales, conv_
                         nc.tensor.transpose(
                             xt[:, u, i * P : (i + 1) * P], words[:, first + i, u, :], identity[:]
                         )
-                banks.append((first, xt))
-            for first, xt in banks:
-                nc.scalar.copy(
-                    out=grouped_words[:, first * P : (first + TILES_PER_BANK) * P, :],
-                    in_=xt[:].rearrange("p u l -> p l u"),
-                )
-            grouped_tiles[r] = grouped
+                xt_tiles[r].append(xt)
+
+        def regroup(r, bank):
+            grouped_words = grouped_tiles[r][:].bitcast(F32).rearrange("p (l u) -> p l u", u=PAIR)
+            columns = TILES_PER_BANK * P
+            nc.scalar.copy(
+                out=grouped_words[:, bank * columns : (bank + 1) * columns, :],
+                in_=xt_tiles[r][bank][:].rearrange("p u l -> p l u"),
+            )
+
+        def transpose_and_regroup(r):
+            transpose(r)
+            regroup(r, 0)
+            regroup(r, 1)
 
         def quantise(r):
             codes = stage.tile([P, ROUND], U32, name="codes", align_bytes=64)
@@ -187,26 +194,32 @@ def tile_conceptembedmodel_pa_t_kernel(tc, x, conv_w_words, conv_w_scales, conv_
         transpose_and_regroup(2)
         for r in range(ROUNDS):
             is_handed = r // ROUNDS_PER_SEQ < HANDED_SEQS
+            subtracted = (r - 2) // 2 if r % 2 == 0 and 0 <= (r - 2) // 2 < HANDED_SEQS else None
+            added = (r - 3) // 2 if r % 2 == 1 and 0 <= (r - 3) // 2 < HANDED_SEQS else None
             if r + X_BUFS < ROUNDS:
                 load(r + X_BUFS)
             if r + 1 < ROUNDS:
                 quantise(r + 1)
-                if r % 2 == 0 and 0 <= (r - 2) // 2 < HANDED_SEQS:
+                if subtracted is not None or added is not None:
                     wait_for_quantise(r + 1)
-                    subtract((r - 2) // 2)
-                if r % 2 == 1 and 0 <= (r - 5) // 2 < HANDED_SEQS:
-                    wait_for_quantise(r + 1)
-                    add((r - 5) // 2)
+            if subtracted is not None:
+                subtract(subtracted)
+            if added is not None:
+                add(added)
+            if r + 1 < ROUNDS:
                 multiply(r + 1, 0)
                 multiply(r + 1, 1)
             if is_handed:
                 hand_over(r)
-            if r % 2 == 1 and 0 <= (r - 3) // 2 < HANDED_SEQS:
-                relu((r - 3) // 2)
             if r + 3 < ROUNDS:
-                transpose_and_regroup(r + 3)
-            if 0 <= (r - 6) // 2 < HANDED_SEQS:
-                take_joined_max((r - 6) // 2, r % 2)
+                transpose(r + 3)
+                regroup(r + 3, 0)
+            if subtracted is not None:
+                relu(subtracted)
+            if r + 3 < ROUNDS:
+                regroup(r + 3, 1)
+            if 0 <= (r - 4) // 2 < HANDED_SEQS:
+                take_joined_max((r - 4) // 2, r % 2)
             take_max(r, 0)
             take_max(r, 1)
             if r + 1 < ROUNDS:
@@ -215,6 +228,9 @@ def tile_conceptembedmodel_pa_t_kernel(tc, x, conv_w_words, conv_w_scales, conv_
             take_max(r, 2)
             if not is_handed:
                 take_max(r, 3)
+        for s in range((ROUNDS - 4) // 2, HANDED_SEQS):
+            take_joined_max(s, 0)
+            take_joined_max(s, 1)
 
         nc.vector.reduce_max(
             out=seq_max[:, 0:RESULT_ROWS].rearrange("p (b t) -> p b t", t=D_TILES),

@@ -30,6 +30,8 @@ RESULT_ROWS = SEQS * D_TILES
 HANDED_TILE = D_TILES - 1
 HANDED_SEQS = 15
 HALF = ROUND // 2
+WARM_PASSES = 6
+HOLD_PASSES = 2
 
 FLOPS = 2 * SEQS * POSITIONS * FEATURES * OUT_FEATURES
 
@@ -157,6 +159,16 @@ def tile_conceptembedmodel_pa_t_kernel(tc, x, conv_w_words, conv_w_scales, conv_
                 axis=AXIS.X,
             )
 
+        def keep_tensor_clock_up(passes):
+            for i in range(passes):
+                unread = z_pool.tile([P, ROUND], F32, name="z")
+                nc.tensor.matmul(
+                    out=unread[:], lhsT=zeros[:, 0:P], rhs=zeros[:], start=True, stop=True
+                )
+
+        zeros = const.tile([P, ROUND], BF16, name="zeros")
+        nc.vector.memset(zeros[:], 0.0)
+        keep_tensor_clock_up(WARM_PASSES)
         w_scales = const.tile([P, OUT_FEATURES], U8, name="w_scales", align_bytes=64)
         nc.vector.memset(w_scales[:].bitcast(I32), 0)
         seq_max = const.tile([P, P], F32, name="seq_max")
@@ -188,6 +200,7 @@ def tile_conceptembedmodel_pa_t_kernel(tc, x, conv_w_words, conv_w_scales, conv_
 
         transpose_and_regroup(0)
         quantise(0)
+        keep_tensor_clock_up(HOLD_PASSES)
         transpose_and_regroup(1)
         for t in range(D_TILES):
             multiply(0, t)

@@ -46,7 +46,7 @@ def tile_conceptembedmodel_pa_t_kernel(tc, x, conv_w_words, conv_w_scales, conv_
         stack.enter_context(tc.manual_schedule())
         const = stack.enter_context(tc.tile_pool(name="const", bufs=1))
         x_pool = stack.enter_context(tc.tile_pool(name="x", bufs=X_BUFS))
-        stage = stack.enter_context(tc.tile_pool(name="stage", bufs=4))
+        stage = stack.enter_context(tc.tile_pool(name="stage", bufs=6))
         xt_pool = stack.enter_context(tc.psum_pool(name="xt", bufs=2))
         z_pool = stack.enter_context(tc.psum_pool(name="z", bufs=6))
         handed = stack.enter_context(tc.tile_pool(name="handed", bufs=4))
@@ -128,27 +128,24 @@ def tile_conceptembedmodel_pa_t_kernel(tc, x, conv_w_words, conv_w_scales, conv_
             nc.scalar.copy(out=half[:], in_=z_tiles[(r, HANDED_TILE)][:])
             half_tiles[(s, h)] = half
 
-        def wait_for_quantise(r):
-            token = handed.tile([P, 1], U32, name="token")
-            nc.gpsimd.tensor_copy(out=token[:], in_=code_tiles[r][0][:, 0:1])
+        def read_by_quantise(r, i):
+            return grouped_tiles[r][:, i * PAIR * ROUND : (i + 1) * PAIR * ROUND].bitcast(F32)
 
-        def subtract(s):
-            difference = handed.tile([P, ROUND], F32, name="difference")
+        def subtract(s, difference):
             nc.gpsimd.tensor_tensor(
-                out=difference[:], in0=half_tiles[(s, 0)][:], in1=half_tiles[(s, 1)][:],
+                out=difference, in0=half_tiles[(s, 0)][:], in1=half_tiles[(s, 1)][:],
                 op=ALU.subtract,
             )
             difference_tiles[s] = difference
 
         def relu(s):
             excess = handed.tile([P, ROUND], F32, name="excess")
-            nc.scalar.activation(out=excess[:], in_=difference_tiles[s][:], func=ACT.Relu)
+            nc.scalar.activation(out=excess[:], in_=difference_tiles[s], func=ACT.Relu)
             excess_tiles[s] = excess
 
-        def add(s):
-            joined = handed.tile([P, ROUND], F32, name="joined")
+        def add(s, joined):
             nc.gpsimd.tensor_tensor(
-                out=joined[:], in0=excess_tiles[s][:], in1=half_tiles[(s, 1)][:], op=ALU.add
+                out=joined, in0=excess_tiles[s][:], in1=half_tiles[(s, 1)][:], op=ALU.add
             )
             joined_tiles[s] = joined
 
@@ -205,34 +202,30 @@ def tile_conceptembedmodel_pa_t_kernel(tc, x, conv_w_words, conv_w_scales, conv_
         for t in range(D_TILES):
             multiply(0, t)
         transpose_and_regroup(2)
+        last = ROUNDS - 1
         for r in range(ROUNDS):
             is_handed = r // ROUNDS_PER_SEQ < HANDED_SEQS
-            subtracted = (r - 2) // 2 if r % 2 == 0 and 0 <= (r - 2) // 2 < HANDED_SEQS else None
-            added = (r - 3) // 2 if r % 2 == 1 and 0 <= (r - 3) // 2 < HANDED_SEQS else None
             if r + X_BUFS < ROUNDS:
                 load(r + X_BUFS)
             if r + 1 < ROUNDS:
                 quantise(r + 1)
-                if subtracted is not None or added is not None:
-                    wait_for_quantise(r + 1)
-            if subtracted is not None:
-                subtract(subtracted)
-            if added is not None:
-                add(added)
+            if r % 2 == 0 and 0 <= (r - 2) // 2 < HANDED_SEQS:
+                subtract((r - 2) // 2, read_by_quantise(r + 1, 0))
+            if r % 2 == 1 and 0 <= (r - 5) // 2 < HANDED_SEQS:
+                add((r - 5) // 2, read_by_quantise(min(r + 1, last), 0))
+            if r == last:
+                add(HANDED_SEQS - 1, read_by_quantise(last, 1))
             if r + 1 < ROUNDS:
                 multiply(r + 1, 0)
                 multiply(r + 1, 1)
             if is_handed:
                 hand_over(r)
+            if r % 2 == 1 and 0 <= (r - 3) // 2 < HANDED_SEQS - 1:
+                relu((r - 3) // 2)
+            if r == last - 1:
+                relu(HANDED_SEQS - 1)
             if r + 3 < ROUNDS:
-                transpose(r + 3)
-                regroup(r + 3, 0)
-            if subtracted is not None:
-                relu(subtracted)
-            if r + 3 < ROUNDS:
-                regroup(r + 3, 1)
-            if 0 <= (r - 4) // 2 < HANDED_SEQS:
-                take_joined_max((r - 4) // 2, r % 2)
+                transpose_and_regroup(r + 3)
             take_max(r, 0)
             take_max(r, 1)
             if r + 1 < ROUNDS:
@@ -241,7 +234,9 @@ def tile_conceptembedmodel_pa_t_kernel(tc, x, conv_w_words, conv_w_scales, conv_
             take_max(r, 2)
             if not is_handed:
                 take_max(r, 3)
-        for s in range((ROUNDS - 4) // 2, HANDED_SEQS):
+            if 0 <= (r - 6) // 2 < HANDED_SEQS:
+                take_joined_max((r - 6) // 2, r % 2)
+        for s in range((ROUNDS - 6) // 2, HANDED_SEQS):
             take_joined_max(s, 0)
             take_joined_max(s, 1)
 

@@ -25,12 +25,13 @@ ROUNDS = SEQS * ROUNDS_PER_SEQ
 D_TILES = OUT_FEATURES // P
 BANK_F32 = 512
 TILES_PER_BANK = BANK_F32 // (PAIR * P)
+BANKS_PER_ROUND = ROW_TILES // TILES_PER_BANK
 X_BUFS = 8
 RESULT_ROWS = SEQS * D_TILES
 HANDED_TILE = D_TILES - 1
 HANDED_SEQS = 15
 HALF = ROUND // 2
-WARM_PASSES = 6
+WARM_PASSES = 3
 HOLD_PASSES = 2
 
 FLOPS = 2 * SEQS * POSITIONS * FEATURES * OUT_FEATURES
@@ -45,7 +46,7 @@ def tile_conceptembedmodel_pa_t_kernel(tc, x, conv_w_words, conv_w_scales, conv_
     with ExitStack() as stack:
         stack.enter_context(tc.manual_schedule())
         const = stack.enter_context(tc.tile_pool(name="const", bufs=1))
-        x_pool = stack.enter_context(tc.tile_pool(name="x", bufs=X_BUFS))
+        x_pool = stack.enter_context(tc.tile_pool(name="x", bufs=X_BUFS * BANKS_PER_ROUND))
         stage = stack.enter_context(tc.tile_pool(name="stage", bufs=6))
         xt_pool = stack.enter_context(tc.psum_pool(name="xt", bufs=2))
         z_pool = stack.enter_context(tc.psum_pool(name="z", bufs=6))
@@ -61,23 +62,30 @@ def tile_conceptembedmodel_pa_t_kernel(tc, x, conv_w_words, conv_w_scales, conv_
         excess_tiles = {}
         joined_tiles = {}
 
+        def load_bank(r, bank):
+            columns = TILES_PER_BANK * FEATURES
+            x_sb = x_pool.tile([P, columns], BF16, name="x_sb")
+            nc.sync.dma_start(
+                out=x_sb[:], in_=x_rounds[r][:, bank * columns : (bank + 1) * columns]
+            )
+            x_tiles[(r, bank)] = x_sb
+
         def load(r):
-            x_sb = x_pool.tile([P, ROW_TILES * FEATURES], BF16, name="x_sb")
-            nc.sync.dma_start(out=x_sb[:], in_=x_rounds[r])
-            x_tiles[r] = x_sb
+            for bank in range(BANKS_PER_ROUND):
+                load_bank(r, bank)
 
         def transpose(r):
-            words = x_tiles[r][:].bitcast(F32).rearrange(
-                "p (j w u) -> p j u w", j=ROW_TILES, u=PAIR
-            )
             grouped_tiles[r] = stage.tile([P, ROUND * PACK], BF16, name="grouped", align_bytes=64)
             xt_tiles[r] = []
-            for first in range(0, ROW_TILES, TILES_PER_BANK):
+            for bank in range(BANKS_PER_ROUND):
+                words = x_tiles[(r, bank)][:].bitcast(F32).rearrange(
+                    "p (j w u) -> p j u w", j=TILES_PER_BANK, u=PAIR
+                )
                 xt = xt_pool.tile([P, PAIR, TILES_PER_BANK * P], F32, name="xt")
                 for i in range(TILES_PER_BANK):
                     for u in range(PAIR):
                         nc.tensor.transpose(
-                            xt[:, u, i * P : (i + 1) * P], words[:, first + i, u, :], identity[:]
+                            xt[:, u, i * P : (i + 1) * P], words[:, i, u, :], identity[:]
                         )
                 xt_tiles[r].append(xt)
 
@@ -178,6 +186,7 @@ def tile_conceptembedmodel_pa_t_kernel(tc, x, conv_w_words, conv_w_scales, conv_
         round_max = const.tile([P, SEQS, D_TILES, ROUNDS_PER_SEQ], F32, name="round_max")
 
         load(0)
+        load(1)
         w_words = const.tile([P, PAIR * OUT_FEATURES], U8, name="w_words", align_bytes=64)
         nc.sync.dma_start(out=w_words[:].bitcast(I32), in_=conv_w_words[0].bitcast(I32))
         for quadrant in range(4):
@@ -185,6 +194,8 @@ def tile_conceptembedmodel_pa_t_kernel(tc, x, conv_w_words, conv_w_scales, conv_
                 out=w_scales[32 * quadrant : 32 * quadrant + 4, :].bitcast(I32),
                 in_=conv_w_scales[0, 4 * quadrant : 4 * quadrant + 4, :].bitcast(I32),
             )
+        for r in range(2, X_BUFS):
+            load(r)
         bias_rows = const.tile([RESULT_ROWS, P], BF16, name="bias_rows")
         nc.sync.dma_start(
             out=bias_rows[:],
@@ -192,8 +203,6 @@ def tile_conceptembedmodel_pa_t_kernel(tc, x, conv_w_words, conv_w_scales, conv_
                 [SEQS, D_TILES, P]
             ),
         )
-        for r in range(1, X_BUFS):
-            load(r)
 
         transpose_and_regroup(0)
         quantise(0)

@@ -220,10 +220,12 @@ def tile_conceptembedmodel_pa_t_kernel(tc, x, conv_w_words, conv_w_scales, conv_
                 quantise(r + 1)
             if r % 2 == 0 and 0 <= (r - 2) // 2 < HANDED_SEQS:
                 subtract((r - 2) // 2, read_by_quantise(r + 1, 0))
-            if r % 2 == 1 and 0 <= (r - 5) // 2 < HANDED_SEQS:
-                add((r - 5) // 2, read_by_quantise(min(r + 1, last), 0))
-            if r == last:
-                add(HANDED_SEQS - 1, read_by_quantise(last, 1))
+            if r % 2 == 1 and 0 <= (r - 5) // 2 < HANDED_SEQS - 2:
+                add((r - 5) // 2, read_by_quantise(r + 1, 0))
+            if r == last - 1:
+                add(HANDED_SEQS - 2, read_by_quantise(last - 2, 0))
+                relu(HANDED_SEQS - 1)
+                add(HANDED_SEQS - 1, read_by_quantise(last - 2, 1))
             if r + 1 < ROUNDS:
                 multiply(r + 1, 0)
                 multiply(r + 1, 1)
@@ -231,8 +233,6 @@ def tile_conceptembedmodel_pa_t_kernel(tc, x, conv_w_words, conv_w_scales, conv_
                 hand_over(r)
             if r % 2 == 1 and 0 <= (r - 3) // 2 < HANDED_SEQS - 1:
                 relu((r - 3) // 2)
-            if r == last - 1:
-                relu(HANDED_SEQS - 1)
             if r + 3 < ROUNDS:
                 transpose_and_regroup(r + 3)
             take_max(r, 0)
@@ -246,8 +246,11 @@ def tile_conceptembedmodel_pa_t_kernel(tc, x, conv_w_words, conv_w_scales, conv_
             if 0 <= (r - 6) // 2 < HANDED_SEQS:
                 take_joined_max((r - 6) // 2, r % 2)
         for s in range((ROUNDS - 6) // 2, HANDED_SEQS):
-            take_joined_max(s, 0)
-            take_joined_max(s, 1)
+            nc.vector.reduce_max(
+                out=round_max[:, s, HANDED_TILE, :],
+                in_=joined_tiles[s].rearrange("p (i c) -> p i c", c=HALF),
+                axis=AXIS.X,
+            )
 
         nc.vector.reduce_max(
             out=seq_max[:, 0:RESULT_ROWS].rearrange("p (b t) -> p b t", t=D_TILES),

@@ -55,6 +55,7 @@ def tile_conceptembedmodel_pa_t_kernel(tc, x, conv_w_words, conv_w_scales, conv_
         x_tiles = {}
         grouped_tiles = {}
         xt_tiles = {}
+        straight_tiles = {}
         code_tiles = {}
         z_tiles = {}
         half_tiles = {}
@@ -74,6 +75,14 @@ def tile_conceptembedmodel_pa_t_kernel(tc, x, conv_w_words, conv_w_scales, conv_
             for bank in range(BANKS_PER_ROUND):
                 load_bank(r, bank)
 
+        def straighten(r):
+            words = x_tiles[(r, BANKS_PER_ROUND - 1)][:].bitcast(F32).rearrange(
+                "p (j w u) -> p j u w", j=TILES_PER_BANK, u=PAIR
+            )
+            straight = stage.tile([P, PAIR, P], F32, name="straight")
+            nc.scalar.copy(out=straight[:], in_=words[:, TILES_PER_BANK - 1, :, :])
+            straight_tiles[r] = straight
+
         def transpose(r):
             grouped_tiles[r] = stage.tile([P, ROUND * PACK], BF16, name="grouped", align_bytes=64)
             xt_tiles[r] = []
@@ -83,9 +92,12 @@ def tile_conceptembedmodel_pa_t_kernel(tc, x, conv_w_words, conv_w_scales, conv_
                 )
                 xt = xt_pool.tile([P, PAIR, TILES_PER_BANK * P], F32, name="xt")
                 for i in range(TILES_PER_BANK):
+                    halves = words[:, i, :, :]
+                    if bank * TILES_PER_BANK + i == ROW_TILES - 1 and r in straight_tiles:
+                        halves = straight_tiles[r][:]
                     for u in range(PAIR):
                         nc.tensor.transpose(
-                            xt[:, u, i * P : (i + 1) * P], words[:, i, u, :], identity[:]
+                            xt[:, u, i * P : (i + 1) * P], halves[:, u, :], identity[:]
                         )
                 xt_tiles[r].append(xt)
 
@@ -211,6 +223,7 @@ def tile_conceptembedmodel_pa_t_kernel(tc, x, conv_w_words, conv_w_scales, conv_
         for t in range(D_TILES):
             multiply(0, t)
         transpose_and_regroup(2)
+        straighten(3)
         last = ROUNDS - 1
         for r in range(ROUNDS):
             is_handed = r // ROUNDS_PER_SEQ < HANDED_SEQS
@@ -235,6 +248,8 @@ def tile_conceptembedmodel_pa_t_kernel(tc, x, conv_w_words, conv_w_scales, conv_
                 relu((r - 3) // 2)
             if r + 3 < ROUNDS:
                 transpose_and_regroup(r + 3)
+            if r + 4 < ROUNDS:
+                straighten(r + 4)
             take_max(r, 0)
             take_max(r, 1)
             if r + 1 < ROUNDS:

@@ -31,7 +31,7 @@ RESULT_ROWS = SEQS * D_TILES
 HANDED_TILE = D_TILES - 1
 HANDED_SEQS = 15
 HALF = ROUND // 2
-WARM_PASSES = 3
+WARM_PASSES = 4
 HOLD_PASSES = 2
 
 FLOPS = 2 * SEQS * POSITIONS * FEATURES * OUT_FEATURES
@@ -63,12 +63,15 @@ def tile_conceptembedmodel_pa_t_kernel(tc, x, conv_w_words, conv_w_scales, conv_
         excess_tiles = {}
         joined_tiles = {}
 
-        def load_bank(r, bank):
+        def load_bank(r, bank, pieces=1):
             columns = TILES_PER_BANK * FEATURES
             x_sb = x_pool.tile([P, columns], BF16, name="x_sb")
-            nc.sync.dma_start(
-                out=x_sb[:], in_=x_rounds[r][:, bank * columns : (bank + 1) * columns]
-            )
+            width = columns // pieces
+            for i in range(pieces):
+                first = bank * columns + i * width
+                nc.sync.dma_start(
+                    out=x_sb[:, i * width : (i + 1) * width], in_=x_rounds[r][:, first : first + width]
+                )
             x_tiles[(r, bank)] = x_sb
 
         def load(r):
@@ -108,6 +111,23 @@ def tile_conceptembedmodel_pa_t_kernel(tc, x, conv_w_words, conv_w_scales, conv_
                 out=grouped_words[:, bank * columns : (bank + 1) * columns, :],
                 in_=xt_tiles[r][bank][:].rearrange("p u l -> p l u"),
             )
+
+        def first_round():
+            grouped_tiles[0] = stage.tile([P, ROUND * PACK], BF16, name="grouped", align_bytes=64)
+            grouped_words = grouped_tiles[0][:].bitcast(F32).rearrange("p (l u) -> p l u", u=PAIR)
+            for j in range(ROW_TILES):
+                bank, i = divmod(j, TILES_PER_BANK)
+                words = x_tiles[(0, bank)][:].bitcast(F32).rearrange(
+                    "p (j w u) -> p j u w", j=TILES_PER_BANK, u=PAIR
+                )
+                xt = z_pool.tile([P, PAIR, P], F32, name="xt_first", tag="z")
+                for u in range(PAIR):
+                    nc.tensor.transpose(xt[:, u, :], words[:, i, u, :], identity[:])
+                copy = nc.scalar.copy if j % 2 == 0 else nc.vector.tensor_copy
+                copy(
+                    out=grouped_words[:, j * P : (j + 1) * P, :],
+                    in_=xt[:].rearrange("p u l -> p l u"),
+                )
 
         def transpose_and_regroup(r):
             transpose(r)
@@ -197,7 +217,8 @@ def tile_conceptembedmodel_pa_t_kernel(tc, x, conv_w_words, conv_w_scales, conv_
         make_identity(nc, identity[:])
         round_max = const.tile([P, SEQS, D_TILES, ROUNDS_PER_SEQ], F32, name="round_max")
 
-        load(0)
+        for bank in range(BANKS_PER_ROUND):
+            load_bank(0, bank, TILES_PER_BANK)
         load(1)
         w_words = const.tile([P, PAIR * OUT_FEATURES], U8, name="w_words", align_bytes=64)
         nc.sync.dma_start(out=w_words[:].bitcast(I32), in_=conv_w_words[0].bitcast(I32))
@@ -216,13 +237,16 @@ def tile_conceptembedmodel_pa_t_kernel(tc, x, conv_w_words, conv_w_scales, conv_
             ),
         )
 
-        transpose_and_regroup(0)
+        first_round()
         quantise(0)
         keep_tensor_clock_up(HOLD_PASSES)
         transpose_and_regroup(1)
-        for t in range(D_TILES):
-            multiply(0, t)
+        multiply(0, 0)
+        multiply(0, 1)
+        multiply(0, 2)
+        take_max(0, 0)
         transpose_and_regroup(2)
+        multiply(0, 3)
         straighten(3)
         last = ROUNDS - 1
         for r in range(ROUNDS):
@@ -250,7 +274,8 @@ def tile_conceptembedmodel_pa_t_kernel(tc, x, conv_w_words, conv_w_scales, conv_
                 transpose_and_regroup(r + 3)
             if r + 4 < ROUNDS:
                 straighten(r + 4)
-            take_max(r, 0)
+            if r > 0:
+                take_max(r, 0)
             take_max(r, 1)
             if r + 1 < ROUNDS:
                 multiply(r + 1, 2)

@@ -31,7 +31,7 @@ RESULT_ROWS = SEQS * D_TILES
 HANDED_TILE = D_TILES - 1
 HANDED_SEQS = 15
 HALF = ROUND // 2
-WARM_PASSES = 4
+WARM_PASSES = 3
 HOLD_PASSES = 2
 
 FLOPS = 2 * SEQS * POSITIONS * FEATURES * OUT_FEATURES
@@ -206,8 +206,6 @@ def tile_conceptembedmodel_pa_t_kernel(tc, x, conv_w_words, conv_w_scales, conv_
         zeros = const.tile([P, ROUND], BF16, name="zeros")
         nc.vector.memset(zeros[:], 0.0)
         keep_tensor_clock_up(WARM_PASSES)
-        w_scales = const.tile([P, OUT_FEATURES], U8, name="w_scales", align_bytes=64)
-        nc.vector.memset(w_scales[:].bitcast(I32), 0)
         seq_max = const.tile([P, P], F32, name="seq_max")
         nc.vector.memset(seq_max[:], 0.0)
         warm = const.tile([P, 1], F32, name="warm")
@@ -217,16 +215,17 @@ def tile_conceptembedmodel_pa_t_kernel(tc, x, conv_w_words, conv_w_scales, conv_
         make_identity(nc, identity[:])
         round_max = const.tile([P, SEQS, D_TILES, ROUNDS_PER_SEQ], F32, name="round_max")
 
-        for bank in range(BANKS_PER_ROUND):
-            load_bank(0, bank, TILES_PER_BANK)
-        load(1)
+        load(0)
         w_words = const.tile([P, PAIR * OUT_FEATURES], U8, name="w_words", align_bytes=64)
         nc.sync.dma_start(out=w_words[:].bitcast(I32), in_=conv_w_words[0].bitcast(I32))
+        w_scales = const.tile([P, OUT_FEATURES], U8, name="w_scales", align_bytes=64)
         for quadrant in range(4):
+            rows = conv_w_scales[:, 4 * quadrant : 4 * quadrant + 4, :].bitcast(I32)
             nc.sync.dma_start(
-                out=w_scales[32 * quadrant : 32 * quadrant + 4, :].bitcast(I32),
-                in_=conv_w_scales[0, 4 * quadrant : 4 * quadrant + 4, :].bitcast(I32),
+                out=w_scales[32 * quadrant : 32 * quadrant + 32, :].bitcast(I32),
+                in_=rows.to_broadcast([8, 4, OUT_FEATURES // 4]),
             )
+        load(1)
         for r in range(2, X_BUFS):
             load(r)
         bias_rows = const.tile([RESULT_ROWS, P], BF16, name="bias_rows")

@@ -31,7 +31,7 @@ RESULT_ROWS = SEQS * D_TILES
 HANDED_TILE = D_TILES - 1
 HANDED_SEQS = 15
 HALF = ROUND // 2
-WARM_PASSES = 3
+WARM_PASSES = 5
 HOLD_PASSES = 2
 
 FLOPS = 2 * SEQS * POSITIONS * FEATURES * OUT_FEATURES
@@ -216,8 +216,6 @@ def tile_conceptembedmodel_pa_t_kernel(tc, x, conv_w_words, conv_w_scales, conv_
         round_max = const.tile([P, SEQS, D_TILES, ROUNDS_PER_SEQ], F32, name="round_max")
 
         load(0)
-        w_words = const.tile([P, PAIR * OUT_FEATURES], U8, name="w_words", align_bytes=64)
-        nc.sync.dma_start(out=w_words[:].bitcast(I32), in_=conv_w_words[0].bitcast(I32))
         w_scales = const.tile([P, OUT_FEATURES], U8, name="w_scales", align_bytes=64)
         for quadrant in range(4):
             rows = conv_w_scales[:, 4 * quadrant : 4 * quadrant + 4, :].bitcast(I32)
@@ -226,6 +224,8 @@ def tile_conceptembedmodel_pa_t_kernel(tc, x, conv_w_words, conv_w_scales, conv_
                 in_=rows.to_broadcast([8, 4, OUT_FEATURES // 4]),
             )
         load(1)
+        w_words = const.tile([P, PAIR * OUT_FEATURES], U8, name="w_words", align_bytes=64)
+        nc.sync.dma_start(out=w_words[:].bitcast(I32), in_=conv_w_words[0].bitcast(I32))
         for r in range(2, X_BUFS):
             load(r)
         bias_rows = const.tile([RESULT_ROWS, P], BF16, name="bias_rows")

@@ -31,7 +31,7 @@ RESULT_ROWS = SEQS * D_TILES
 HANDED_TILE = D_TILES - 1
 HANDED_SEQS = 15
 HALF = ROUND // 2
-WARM_PASSES = 5
+WARM_PASSES = 4
 HOLD_PASSES = 2
 
 FLOPS = 2 * SEQS * POSITIONS * FEATURES * OUT_FEATURES
@@ -46,11 +46,12 @@ def tile_conceptembedmodel_pa_t_kernel(tc, x, conv_w_words, conv_w_scales, conv_
     with ExitStack() as stack:
         stack.enter_context(tc.manual_schedule())
         const = stack.enter_context(tc.tile_pool(name="const", bufs=1))
-        x_pool = stack.enter_context(tc.tile_pool(name="x", bufs=X_BUFS * BANKS_PER_ROUND))
+        x_pool = stack.enter_context(tc.tile_pool(name="x", bufs=X_BUFS))
         stage = stack.enter_context(tc.tile_pool(name="stage", bufs=6))
         xt_pool = stack.enter_context(tc.psum_pool(name="xt", bufs=2))
         z_pool = stack.enter_context(tc.psum_pool(name="z", bufs=6))
         handed = stack.enter_context(tc.tile_pool(name="handed", bufs=4))
+        unread_pool = stack.enter_context(tc.tile_pool(name="unread", bufs=2))
 
         x_tiles = {}
         grouped_tiles = {}
@@ -63,20 +64,15 @@ def tile_conceptembedmodel_pa_t_kernel(tc, x, conv_w_words, conv_w_scales, conv_
         excess_tiles = {}
         joined_tiles = {}
 
-        def load_bank(r, bank, pieces=1):
-            columns = TILES_PER_BANK * FEATURES
-            x_sb = x_pool.tile([P, columns], BF16, name="x_sb")
-            width = columns // pieces
+        def load(r, pieces=1):
+            x_sb = x_pool.tile([P, ROW_TILES * FEATURES], BF16, name="x_sb")
+            width = ROW_TILES * FEATURES // pieces
             for i in range(pieces):
-                first = bank * columns + i * width
-                nc.sync.dma_start(
-                    out=x_sb[:, i * width : (i + 1) * width], in_=x_rounds[r][:, first : first + width]
-                )
-            x_tiles[(r, bank)] = x_sb
-
-        def load(r):
+                columns = slice(i * width, (i + 1) * width)
+                nc.sync.dma_start(out=x_sb[:, columns], in_=x_rounds[r][:, columns])
+            half = TILES_PER_BANK * FEATURES
             for bank in range(BANKS_PER_ROUND):
-                load_bank(r, bank)
+                x_tiles[(r, bank)] = x_sb[:, bank * half : (bank + 1) * half]
 
         def straighten(r):
             words = x_tiles[(r, BANKS_PER_ROUND - 1)][:].bitcast(F32).rearrange(
@@ -168,6 +164,15 @@ def tile_conceptembedmodel_pa_t_kernel(tc, x, conv_w_words, conv_w_scales, conv_
             nc.scalar.copy(out=half[:], in_=z_tiles[(r, HANDED_TILE)][:])
             half_tiles[(s, h)] = half
 
+        def finish_max(t):
+            column = final * D_TILES + t
+            unread = unread_pool.tile([P, ROUND], F32, name="unread_sum")
+            nc.vector.tensor_scalar(
+                out=unread[:], in0=z_tiles[(last, t)][:], scalar1=bias[:, t : t + 1],
+                scalar2=last_start[:, t - 2 : t - 1], op0=ALU.add, op1=ALU.max,
+                accum_out=seq_max[:, column : column + 1],
+            )
+
         def read_by_quantise(r, i):
             return grouped_tiles[r][:, i * PAIR * ROUND : (i + 1) * PAIR * ROUND].bitcast(F32)
 
@@ -214,8 +219,10 @@ def tile_conceptembedmodel_pa_t_kernel(tc, x, conv_w_words, conv_w_scales, conv_
         identity = const.tile([P, P], F32, name="identity")
         make_identity(nc, identity[:])
         round_max = const.tile([P, SEQS, D_TILES, ROUNDS_PER_SEQ], F32, name="round_max")
+        early_max = const.tile([P, RESULT_ROWS - 2], F32, name="early_max")
+        last_start = const.tile([P, 2], F32, name="last_start")
 
-        load(0)
+        load(0, BANKS_PER_ROUND)
         w_scales = const.tile([P, OUT_FEATURES], U8, name="w_scales", align_bytes=64)
         for quadrant in range(4):
             rows = conv_w_scales[:, 4 * quadrant : 4 * quadrant + 4, :].bitcast(I32)
@@ -228,13 +235,8 @@ def tile_conceptembedmodel_pa_t_kernel(tc, x, conv_w_words, conv_w_scales, conv_
         nc.sync.dma_start(out=w_words[:].bitcast(I32), in_=conv_w_words[0].bitcast(I32))
         for r in range(2, X_BUFS):
             load(r)
-        bias_rows = const.tile([RESULT_ROWS, P], BF16, name="bias_rows")
-        nc.sync.dma_start(
-            out=bias_rows[:],
-            in_=conv_b.rearrange("(o t d) -> o t d", o=1, t=D_TILES).to_broadcast(
-                [SEQS, D_TILES, P]
-            ),
-        )
+        bias_raw = const.tile([P, D_TILES], BF16, name="bias_raw")
+        bias = const.tile([P, RESULT_ROWS], F32, name="bias")
 
         first_round()
         quantise(0)
@@ -248,12 +250,16 @@ def tile_conceptembedmodel_pa_t_kernel(tc, x, conv_w_words, conv_w_scales, conv_
         multiply(0, 3)
         straighten(3)
         last = ROUNDS - 1
-        for r in range(ROUNDS):
+        for r in range(ROUNDS - 1):
             is_handed = r // ROUNDS_PER_SEQ < HANDED_SEQS
             if r + X_BUFS < ROUNDS:
                 load(r + X_BUFS)
-            if r + 1 < ROUNDS:
-                quantise(r + 1)
+            if r == ROUNDS - X_BUFS:
+                with nc.allow_non_contiguous_dma(reason="512 bias values, one to a partition"):
+                    nc.sync.dma_start(
+                        out=bias_raw[:], in_=conv_b.rearrange("(t p) -> p t", t=D_TILES)
+                    )
+            quantise(r + 1)
             if r % 2 == 0 and 0 <= (r - 2) // 2 < HANDED_SEQS:
                 subtract((r - 2) // 2, read_by_quantise(r + 1, 0))
             if r % 2 == 1 and 0 <= (r - 5) // 2 < HANDED_SEQS - 2:
@@ -262,9 +268,8 @@ def tile_conceptembedmodel_pa_t_kernel(tc, x, conv_w_words, conv_w_scales, conv_
                 add(HANDED_SEQS - 2, read_by_quantise(last - 2, 0))
                 relu(HANDED_SEQS - 1)
                 add(HANDED_SEQS - 1, read_by_quantise(last - 2, 1))
-            if r + 1 < ROUNDS:
-                multiply(r + 1, 0)
-                multiply(r + 1, 1)
+            multiply(r + 1, 0)
+            multiply(r + 1, 1)
             if is_handed:
                 hand_over(r)
             if r % 2 == 1 and 0 <= (r - 3) // 2 < HANDED_SEQS - 1:
@@ -273,41 +278,58 @@ def tile_conceptembedmodel_pa_t_kernel(tc, x, conv_w_words, conv_w_scales, conv_
                 transpose_and_regroup(r + 3)
             if r + 4 < ROUNDS:
                 straighten(r + 4)
+            if r == ROUNDS - 4:
+                nc.scalar.copy(
+                    out=bias[:].rearrange("p (b t) -> p b t", t=D_TILES),
+                    in_=bias_raw[:].rearrange("p (o t) -> p o t", o=1).to_broadcast(
+                        [P, SEQS, D_TILES]
+                    ),
+                )
             if r > 0:
                 take_max(r, 0)
             take_max(r, 1)
-            if r + 1 < ROUNDS:
-                multiply(r + 1, 2)
-                multiply(r + 1, 3)
+            multiply(r + 1, 2)
+            multiply(r + 1, 3)
             take_max(r, 2)
             if not is_handed:
                 take_max(r, 3)
             if 0 <= (r - 6) // 2 < HANDED_SEQS:
                 take_joined_max((r - 6) // 2, r % 2)
+        final = SEQS - 1
+        early_columns = RESULT_ROWS - 2
+        take_max(last, 0)
+        for t in (2, 3):
+            nc.scalar.activation(
+                out=last_start[:, t - 2 : t - 1], in_=round_max[:, final, t, 0:1], func=ACT.Identity,
+                bias=bias[:, t : t + 1],
+            )
+        take_joined_max((last - 6) // 2, last % 2)
+        take_max(last, 1)
         for s in range((ROUNDS - 6) // 2, HANDED_SEQS):
             nc.vector.reduce_max(
                 out=round_max[:, s, HANDED_TILE, :],
                 in_=joined_tiles[s].rearrange("p (i c) -> p i c", c=HALF),
                 axis=AXIS.X,
             )
-
+        finish_max(2)
         nc.vector.reduce_max(
-            out=seq_max[:, 0:RESULT_ROWS].rearrange("p (b t) -> p b t", t=D_TILES),
-            in_=round_max[:],
+            out=early_max[:],
+            in_=round_max[:].rearrange("p b t h -> p (b t) h")[:, 0:early_columns, :],
             axis=AXIS.X,
+        )
+        finish_max(3)
+        nc.vector.tensor_tensor(
+            out=seq_max[:, 0:early_columns], in0=early_max[:], in1=bias[:, 0:early_columns], op=ALU.add
         )
         rows = xt_pool.tile([P, P], F32, name="rows", tag="xt")
         nc.tensor.transpose(rows[:], seq_max[:], identity[:])
-        v = const.tile([RESULT_ROWS, P], F32, name="v")
-        nc.vector.tensor_tensor(out=v[:], in0=rows[0:RESULT_ROWS, :], in1=bias_rows[:], op=ALU.add)
         negative = const.tile([RESULT_ROWS, P], F32, name="negative")
-        nc.vector.tensor_scalar_min(negative[:], v[:], 0.0)
+        nc.vector.tensor_scalar_min(negative[:], rows[0:RESULT_ROWS, :], 0.0)
         grown = const.tile([RESULT_ROWS, P], F32, name="grown")
         nc.scalar.activation(out=grown[:], in_=negative[:], func=ACT.Exp)
-        positive = const.tile([RESULT_ROWS, P], F32, name="positive")
-        nc.vector.tensor_scalar_max(positive[:], v[:], 0.0)
         result = const.tile([RESULT_ROWS, P], F32, name="result")
         nc.vector.scalar_tensor_tensor(
-            out=result[:], in0=grown[:], scalar=-1.0, in1=positive[:], op0=ALU.add, op1=ALU.add
+            out=result[:], in0=grown[:], scalar=-1.0, in1=rows[0:RESULT_ROWS, :],
+            op0=ALU.add, op1=ALU.max,
         )
         nc.sync.dma_start(out=out.rearrange("b (t d) -> (b t) d", t=D_TILES), in_=result[:])

@@ -209,7 +209,7 @@ def tile_conceptembedmodel_pa_t_kernel(tc, x, conv_w_words, conv_w_scales, conv_
                 )
 
         zeros = const.tile([P, ROUND], BF16, name="zeros")
-        nc.vector.memset(zeros[:], 0.0)
+        nc.gpsimd.memset(zeros[:].bitcast(F32), 0.0)
         keep_tensor_clock_up(WARM_PASSES)
         seq_max = const.tile([P, P], F32, name="seq_max")
         nc.vector.memset(seq_max[:], 0.0)
@@ -223,6 +223,9 @@ def tile_conceptembedmodel_pa_t_kernel(tc, x, conv_w_words, conv_w_scales, conv_
         last_start = const.tile([P, 2], F32, name="last_start")
 
         load(0, BANKS_PER_ROUND)
+        load(1)
+        w_words = const.tile([P, PAIR * OUT_FEATURES], U8, name="w_words", align_bytes=64)
+        nc.sync.dma_start(out=w_words[:].bitcast(I32), in_=conv_w_words[0].bitcast(I32))
         w_scales = const.tile([P, OUT_FEATURES], U8, name="w_scales", align_bytes=64)
         for quadrant in range(4):
             rows = conv_w_scales[:, 4 * quadrant : 4 * quadrant + 4, :].bitcast(I32)
@@ -230,9 +233,6 @@ def tile_conceptembedmodel_pa_t_kernel(tc, x, conv_w_words, conv_w_scales, conv_
                 out=w_scales[32 * quadrant : 32 * quadrant + 32, :].bitcast(I32),
                 in_=rows.to_broadcast([8, 4, OUT_FEATURES // 4]),
             )
-        load(1)
-        w_words = const.tile([P, PAIR * OUT_FEATURES], U8, name="w_words", align_bytes=64)
-        nc.sync.dma_start(out=w_words[:].bitcast(I32), in_=conv_w_words[0].bitcast(I32))
         for r in range(2, X_BUFS):
             load(r)
         bias_raw = const.tile([P, D_TILES], BF16, name="bias_raw")

@@ -321,15 +321,20 @@ def tile_conceptembedmodel_pa_t_kernel(tc, x, conv_w_words, conv_w_scales, conv_
         nc.vector.tensor_tensor(
             out=seq_max[:, 0:early_columns], in0=early_max[:], in1=bias[:, 0:early_columns], op=ALU.add
         )
-        rows = xt_pool.tile([P, P], F32, name="rows", tag="xt")
-        nc.tensor.transpose(rows[:], seq_max[:], identity[:])
-        negative = const.tile([RESULT_ROWS, P], F32, name="negative")
-        nc.vector.tensor_scalar_min(negative[:], rows[0:RESULT_ROWS, :], 0.0)
+        rows = []
+        for i in range(2):
+            bank = xt_pool.tile([P, P], F32, name="rows", tag="xt")
+            nc.tensor.transpose(bank[:], seq_max[:], identity[:])
+            rows.append(bank)
         grown = const.tile([RESULT_ROWS, P], F32, name="grown")
-        nc.scalar.activation(out=grown[:], in_=negative[:], func=ACT.Exp)
+        nc.scalar.activation(out=grown[:], in_=rows[0][0:RESULT_ROWS, :], func=ACT.Exp)
+        above = const.tile([RESULT_ROWS, P], F32, name="above")
+        nc.vector.tensor_scalar(
+            out=above[:], in0=rows[1][0:RESULT_ROWS, :], scalar1=0.0, scalar2=-1.0,
+            op0=ALU.max, op1=ALU.add,
+        )
         result = const.tile([RESULT_ROWS, P], F32, name="result")
         nc.vector.scalar_tensor_tensor(
-            out=result[:], in0=grown[:], scalar=-1.0, in1=rows[0:RESULT_ROWS, :],
-            op0=ALU.add, op1=ALU.max,
+            out=result[:], in0=grown[:], scalar=1.0, in1=above[:], op0=ALU.min, op1=ALU.add
         )
         nc.sync.dma_start(out=out.rearrange("b (t d) -> (b t) d", t=D_TILES), in_=result[:])

from contextlib import ExitStack

import concourse.mybir as mybir
from concourse.masks import make_identity

F32 = mybir.dt.float32
BF16 = mybir.dt.bfloat16
I32 = mybir.dt.int32
U32 = mybir.dt.uint32
U8 = mybir.dt.uint8
FP8X4 = mybir.dt.float8_e4m3fn_x4
FP4X4 = mybir.dt.float4_e2m1fn_x4
ALU = mybir.AluOpType
ACT = mybir.ActivationFunctionType
AXIS = mybir.AxisListType

SEQS, POSITIONS, FEATURES, OUT_FEATURES = 16, 1024, 512, 512
P = 128
PACK = 4
PAIR = 2
ROUND = 512
ROW_TILES = ROUND // P
ROUNDS_PER_SEQ = POSITIONS // ROUND
ROUNDS = SEQS * ROUNDS_PER_SEQ
D_TILES = OUT_FEATURES // P
BANK_F32 = 512
TILES_PER_BANK = BANK_F32 // (PAIR * P)
BANKS_PER_ROUND = ROW_TILES // TILES_PER_BANK
X_BUFS = 8
RESULT_ROWS = SEQS * D_TILES
HANDED_TILE = D_TILES - 1
HANDED_SEQS = 15
HALF = ROUND // 2
WARM_PASSES = 4
HOLD_PASSES = 2

FLOPS = 2 * SEQS * POSITIONS * FEATURES * OUT_FEATURES


def tile_conceptembedmodel_pa_t_kernel(tc, x, conv_w_words, conv_w_scales, conv_b, out):
    nc = tc.nc
    x_rounds = x.rearrange(
        "b (h p j) f -> (b h) p (j f)", h=ROUNDS_PER_SEQ, p=P, j=ROW_TILES
    )

    with ExitStack() as stack:
        stack.enter_context(tc.manual_schedule())
        const = stack.enter_context(tc.tile_pool(name="const", bufs=1))
        x_pool = stack.enter_context(tc.tile_pool(name="x", bufs=X_BUFS))
        stage = stack.enter_context(tc.tile_pool(name="stage", bufs=6))
        xt_pool = stack.enter_context(tc.psum_pool(name="xt", bufs=2))
        z_pool = stack.enter_context(tc.psum_pool(name="z", bufs=6))
        handed = stack.enter_context(tc.tile_pool(name="handed", bufs=4))
        unread_pool = stack.enter_context(tc.tile_pool(name="unread", bufs=2))

        x_tiles = {}
        grouped_tiles = {}
        xt_tiles = {}
        straight_tiles = {}
        code_tiles = {}
        z_tiles = {}
        half_tiles = {}
        difference_tiles = {}
        excess_tiles = {}
        joined_tiles = {}

        def load(r, pieces=1):
            x_sb = x_pool.tile([P, ROW_TILES * FEATURES], BF16, name="x_sb")
            width = ROW_TILES * FEATURES // pieces
            for i in range(pieces):
                columns = slice(i * width, (i + 1) * width)
                nc.sync.dma_start(out=x_sb[:, columns], in_=x_rounds[r][:, columns])
            half = TILES_PER_BANK * FEATURES
            for bank in range(BANKS_PER_ROUND):
                x_tiles[(r, bank)] = x_sb[:, bank * half : (bank + 1) * half]

        def straighten(r):
            words = x_tiles[(r, BANKS_PER_ROUND - 1)][:].bitcast(F32).rearrange(
                "p (j w u) -> p j u w", j=TILES_PER_BANK, u=PAIR
            )
            straight = stage.tile([P, PAIR, P], F32, name="straight")
            nc.scalar.copy(out=straight[:], in_=words[:, TILES_PER_BANK - 1, :, :])
            straight_tiles[r] = straight

        def transpose(r):
            grouped_tiles[r] = stage.tile([P, ROUND * PACK], BF16, name="grouped", align_bytes=64)
            xt_tiles[r] = []
            for bank in range(BANKS_PER_ROUND):
                words = x_tiles[(r, bank)][:].bitcast(F32).rearrange(
                    "p (j w u) -> p j u w", j=TILES_PER_BANK, u=PAIR
                )
                xt = xt_pool.tile([P, PAIR, TILES_PER_BANK * P], F32, name="xt")
                for i in range(TILES_PER_BANK):
                    halves = words[:, i, :, :]
                    if bank * TILES_PER_BANK + i == ROW_TILES - 1 and r in straight_tiles:
                        halves = straight_tiles[r][:]
                    for u in range(PAIR):
                        nc.tensor.transpose(
                            xt[:, u, i * P : (i + 1) * P], halves[:, u, :], identity[:]
                        )
                xt_tiles[r].append(xt)

        def regroup(r, bank):
            grouped_words = grouped_tiles[r][:].bitcast(F32).rearrange("p (l u) -> p l u", u=PAIR)
            columns = TILES_PER_BANK * P
            nc.scalar.copy(
                out=grouped_words[:, bank * columns : (bank + 1) * columns, :],
                in_=xt_tiles[r][bank][:].rearrange("p u l -> p l u"),
            )

        def first_round():
            grouped_tiles[0] = stage.tile([P, ROUND * PACK], BF16, name="grouped", align_bytes=64)
            grouped_words = grouped_tiles[0][:].bitcast(F32).rearrange("p (l u) -> p l u", u=PAIR)
            for j in range(ROW_TILES):
                bank, i = divmod(j, TILES_PER_BANK)
                words = x_tiles[(0, bank)][:].bitcast(F32).rearrange(
                    "p (j w u) -> p j u w", j=TILES_PER_BANK, u=PAIR
                )
                xt = z_pool.tile([P, PAIR, P], F32, name="xt_first", tag="z")
                for u in range(PAIR):
                    nc.tensor.transpose(xt[:, u, :], words[:, i, u, :], identity[:])
                copy = nc.scalar.copy if j % 2 == 0 else nc.vector.tensor_copy
                copy(
                    out=grouped_words[:, j * P : (j + 1) * P, :],
                    in_=xt[:].rearrange("p u l -> p l u"),
                )

        def transpose_and_regroup(r):
            transpose(r)
            regroup(r, 0)
            regroup(r, 1)

        def quantise(r):
            codes = stage.tile([P, ROUND], U32, name="codes", align_bytes=64)
            scales = stage.tile([P, ROUND], U8, name="scales", align_bytes=64)
            nc.vector.quantize_mx(
                out=codes[:].bitcast(FP8X4), scales=scales[:], in_=grouped_tiles[r][:]
            )
            code_tiles[r] = (codes, scales)

        def multiply(r, t):
            codes, scales = code_tiles[r]
            z = z_pool.tile([P, ROUND], F32, name="z")
            nc.tensor.matmul_mx(
                out=z[:],
                lhsT=w_words[:, t * PAIR * P : (t + 1) * PAIR * P].bitcast(FP4X4),
                lhsT_scale=w_scales[:, t * P : (t + 1) * P],
                rhs=codes[:].bitcast(FP8X4),
                rhs_scale=scales[:],
                start=True,
                stop=True,
            )
            z_tiles[(r, t)] = z

        def take_max(r, t):
            b, h = divmod(r, ROUNDS_PER_SEQ)
            nc.vector.reduce_max(
                out=round_max[:, b, t, h : h + 1], in_=z_tiles[(r, t)][:], axis=AXIS.X
            )

        def hand_over(r):
            s, h = divmod(r, ROUNDS_PER_SEQ)
            half = handed.tile([P, ROUND], F32, name="half%d" % h)
            nc.scalar.copy(out=half[:], in_=z_tiles[(r, HANDED_TILE)][:])
            half_tiles[(s, h)] = half

        def finish_max(t):
            column = final * D_TILES + t
            unread = unread_pool.tile([P, ROUND], F32, name="unread_sum")
            nc.vector.tensor_scalar(
                out=unread[:], in0=z_tiles[(last, t)][:], scalar1=bias[:, t : t + 1],
                scalar2=last_start[:, t - 2 : t - 1], op0=ALU.add, op1=ALU.max,
                accum_out=seq_max[:, column : column + 1],
            )

        def read_by_quantise(r, i):
            return grouped_tiles[r][:, i * PAIR * ROUND : (i + 1) * PAIR * ROUND].bitcast(F32)

        def subtract(s, difference):
            nc.gpsimd.tensor_tensor(
                out=difference, in0=half_tiles[(s, 0)][:], in1=half_tiles[(s, 1)][:],
                op=ALU.subtract,
            )
            difference_tiles[s] = difference

        def relu(s):
            excess = handed.tile([P, ROUND], F32, name="excess")
            nc.scalar.activation(out=excess[:], in_=difference_tiles[s], func=ACT.Relu)
            excess_tiles[s] = excess

        def add(s, joined):
            nc.gpsimd.tensor_tensor(
                out=joined, in0=excess_tiles[s][:], in1=half_tiles[(s, 1)][:], op=ALU.add
            )
            joined_tiles[s] = joined

        def take_joined_max(s, i):
            nc.vector.reduce_max(
                out=round_max[:, s, HANDED_TILE, i : i + 1],
                in_=joined_tiles[s][:, i * HALF : (i + 1) * HALF],
                axis=AXIS.X,
            )

        def keep_tensor_clock_up(passes):
            for i in range(passes):
                unread = z_pool.tile([P, ROUND], F32, name="z")
                nc.tensor.matmul(
                    out=unread[:], lhsT=zeros[:, 0:P], rhs=zeros[:], start=True, stop=True
                )

        zeros = const.tile([P, ROUND], BF16, name="zeros")
        nc.gpsimd.memset(zeros[:].bitcast(F32), 0.0)
        keep_tensor_clock_up(WARM_PASSES)
        seq_max = const.tile([P, P], F32, name="seq_max")
        nc.vector.memset(seq_max[:], 0.0)
        warm = const.tile([P, 1], F32, name="warm")
        nc.vector.memset(warm[:], 0.0)
        nc.scalar.activation(out=warm[:], in_=warm[:], func=ACT.Exp)
        identity = const.tile([P, P], F32, name="identity")
        make_identity(nc, identity[:])
        round_max = const.tile([P, SEQS, D_TILES, ROUNDS_PER_SEQ], F32, name="round_max")
        early_max = const.tile([P, RESULT_ROWS - 2], F32, name="early_max")
        last_start = const.tile([P, 2], F32, name="last_start")

        load(0, BANKS_PER_ROUND)
        load(1)
        w_words = const.tile([P, PAIR * OUT_FEATURES], U8, name="w_words", align_bytes=64)
        nc.sync.dma_start(out=w_words[:].bitcast(I32), in_=conv_w_words[0].bitcast(I32))
        w_scales = const.tile([P, OUT_FEATURES], U8, name="w_scales", align_bytes=64)
        for quadrant in range(4):
            rows = conv_w_scales[:, 4 * quadrant : 4 * quadrant + 4, :].bitcast(I32)
            nc.sync.dma_start(
                out=w_scales[32 * quadrant : 32 * quadrant + 32, :].bitcast(I32),
                in_=rows.to_broadcast([8, 4, OUT_FEATURES // 4]),
            )
        for r in range(2, X_BUFS):
            load(r)
        bias_raw = const.tile([P, D_TILES], BF16, name="bias_raw")
        bias = const.tile([P, RESULT_ROWS], F32, name="bias")

        first_round()
        quantise(0)
        keep_tensor_clock_up(HOLD_PASSES)
        transpose_and_regroup(1)
        multiply(0, 0)
        multiply(0, 1)
        multiply(0, 2)
        take_max(0, 0)
        transpose_and_regroup(2)
        multiply(0, 3)
        straighten(3)
        last = ROUNDS - 1
        for r in range(ROUNDS - 1):
            is_handed = r // ROUNDS_PER_SEQ < HANDED_SEQS
            if r + X_BUFS < ROUNDS:
                load(r + X_BUFS)
            if r == ROUNDS - X_BUFS:
                with nc.allow_non_contiguous_dma(reason="512 bias values, one to a partition"):
                    nc.sync.dma_start(
                        out=bias_raw[:], in_=conv_b.rearrange("(t p) -> p t", t=D_TILES)
                    )
            quantise(r + 1)
            if r % 2 == 0 and 0 <= (r - 2) // 2 < HANDED_SEQS:
                subtract((r - 2) // 2, read_by_quantise(r + 1, 0))
            if r % 2 == 1 and 0 <= (r - 5) // 2 < HANDED_SEQS - 2:
                add((r - 5) // 2, read_by_quantise(r + 1, 0))
            if r == last - 1:
                add(HANDED_SEQS - 2, read_by_quantise(last - 2, 0))
                relu(HANDED_SEQS - 1)
                add(HANDED_SEQS - 1, read_by_quantise(last - 2, 1))
            multiply(r + 1, 0)
            multiply(r + 1, 1)
            if is_handed:
                hand_over(r)
            if r % 2 == 1 and 0 <= (r - 3) // 2 < HANDED_SEQS - 1:
                relu((r - 3) // 2)
            if r + 3 < ROUNDS:
                transpose_and_regroup(r + 3)
            if r + 4 < ROUNDS:
                straighten(r + 4)
            if r == ROUNDS - 4:
                nc.scalar.copy(
                    out=bias[:].rearrange("p (b t) -> p b t", t=D_TILES),
                    in_=bias_raw[:].rearrange("p (o t) -> p o t", o=1).to_broadcast(
                        [P, SEQS, D_TILES]
                    ),
                )
            if r > 0:
                take_max(r, 0)
            take_max(r, 1)
            multiply(r + 1, 2)
            multiply(r + 1, 3)
            take_max(r, 2)
            if not is_handed:
                take_max(r, 3)
            if 0 <= (r - 6) // 2 < HANDED_SEQS:
                take_joined_max((r - 6) // 2, r % 2)
        final = SEQS - 1
        early_columns = RESULT_ROWS - 2
        take_max(last, 0)
        for t in (2, 3):
            nc.scalar.activation(
                out=last_start[:, t - 2 : t - 1], in_=round_max[:, final, t, 0:1], func=ACT.Identity,
                bias=bias[:, t : t + 1],
            )
        take_joined_max((last - 6) // 2, last % 2)
        take_max(last, 1)
        for s in range((ROUNDS - 6) // 2, HANDED_SEQS):
            nc.vector.reduce_max(
                out=round_max[:, s, HANDED_TILE, :],
                in_=joined_tiles[s].rearrange("p (i c) -> p i c", c=HALF),
                axis=AXIS.X,
            )
        finish_max(2)
        nc.vector.reduce_max(
            out=early_max[:],
            in_=round_max[:].rearrange("p b t h -> p (b t) h")[:, 0:early_columns, :],
            axis=AXIS.X,
        )
        finish_max(3)
        nc.vector.tensor_tensor(
            out=seq_max[:, 0:early_columns], in0=early_max[:], in1=bias[:, 0:early_columns], op=ALU.add
        )
        rows = []
        for i in range(2):
            bank = xt_pool.tile([P, P], F32, name="rows", tag="xt")
            nc.tensor.transpose(bank[:], seq_max[:], identity[:])
            rows.append(bank)
        grown = const.tile([RESULT_ROWS, P], F32, name="grown")
        nc.scalar.activation(out=grown[:], in_=rows[0][0:RESULT_ROWS, :], func=ACT.Exp)
        above = const.tile([RESULT_ROWS, P], F32, name="above")
        nc.vector.tensor_scalar(
            out=above[:], in0=rows[1][0:RESULT_ROWS, :], scalar1=0.0, scalar2=-1.0,
            op0=ALU.max, op1=ALU.add,
        )
        result = const.tile([RESULT_ROWS, P], F32, name="result")
        nc.vector.scalar_tensor_tensor(
            out=result[:], in0=grown[:], scalar=1.0, in1=above[:], op0=ALU.min, op1=ALU.add
        )
        nc.sync.dma_start(out=out.rearrange("b (t d) -> (b t) d", t=D_TILES), in_=result[:])
